import numpy as np
import ml_dtypes


def mxq(x, axis, fmt="e4m3"):
    dtype, down = {"e4m3": (ml_dtypes.float8_e4m3fn, 7), "e5m2": (ml_dtypes.float8_e5m2, 14)}[fmt]
    v = np.moveaxis(np.asarray(x, np.float32).astype(ml_dtypes.bfloat16).astype(np.float64), axis, -1)
    blocks = v.reshape(v.shape[:-1] + (-1, 32))
    amax = np.abs(blocks).max(-1, keepdims=True)
    byte = np.maximum(np.where(amax > 0, np.frexp(amax)[1] - 1 + 127, 0) - down, 1)
    scale = np.exp2(byte - 127.0)
    codes = (blocks / scale).astype(np.float32).astype(dtype).astype(np.float64)
    return np.moveaxis((codes * scale).reshape(v.shape), -1, axis)


WIDE = False


def mx_kscale(k):
    if not WIDE:
        return np.ones(k)
    levels = np.array([10, -10, 5, -5, 0])
    a = np.random.permutation(np.resize(levels, k // 512 * 4)).reshape(k // 512, 4)
    idx = np.arange(k)
    return np.exp2(a[idx // 512, idx % 128 // 32])


BF16 = ml_dtypes.bfloat16


def bf(x):
    return np.asarray(x, np.float32).astype(BF16)


def f64(x):
    return np.asarray(x).astype(np.float64)


B, D, R = 2048, 2048, 128


def softplus(v):
    return np.log1p(np.exp(v))


def setup_inputs():
    s = mx_kscale(D)
    w = 1.0 / np.sqrt(D)
    return {"x": bf(np.random.standard_normal((B, D)) * s),
            "state_re": bf(np.random.standard_normal((B, R))),
            "state_im": bf(np.random.standard_normal((B, R))),
            "W_dt": bf(np.random.standard_normal((R, D)) * 0.5 * w / s),
            "b_dt": bf(np.random.standard_normal(R) * 0.3),
            "W_ph": bf(np.random.standard_normal((R, D)) * 0.5 * w / s),
            "b_ph": bf(np.random.standard_normal(R) * 0.3),
            "W_B": bf(np.random.standard_normal((R, D)) * w / s),
            "A_real": bf(np.random.standard_normal(R) * 0.5),
            "A_imag": bf(np.random.standard_normal(R) * 0.5)}


def reference(x, state_re, state_im, W_dt, b_dt, W_ph, b_ph, W_B, A_real, A_imag):
    xq = mxq(f64(x), 1, "e4m3")
    dt = softplus((xq @ mxq(f64(W_dt), 1, "e4m3").T) + f64(b_dt))
    phase = np.tanh((xq @ mxq(f64(W_ph), 1, "e4m3").T) + f64(b_ph)) * np.pi
    decay = np.exp(-dt * np.exp(f64(A_real)))
    angle = dt * f64(A_imag) + phase
    B_val = xq @ mxq(f64(W_B), 1, "e4m3").T
    cos = np.cos(angle)
    sin = np.sin(angle)
    new_re = (f64(state_re) * cos - f64(state_im) * sin) * decay + B_val
    new_im = (f64(state_re) * sin + f64(state_im) * cos) * decay
    return new_re, new_im

@@ -1,0 +1,276 @@
+import math
+from contextlib import ExitStack
+
+import concourse.mybir as mybir
+from concourse.masks import make_identity
+
+F32 = mybir.dt.float32
+BF16 = mybir.dt.bfloat16
+U32 = mybir.dt.uint32
+U8 = mybir.dt.uint8
+FP8X4 = mybir.dt.float8_e4m3fn_x4
+ACT = mybir.ActivationFunctionType
+ALU = mybir.AluOpType
+
+B, D, R = 2048, 2048, 128
+FLOPS = 2 * B * D * 3 * R
+
+P = 128
+PACK = 4
+K_PASS = P * PACK
+PASSES = D // K_PASS
+WORDS_PASS = K_PASS // 2
+
+ROW_TILES = B // P
+PIECE_TILES = 2
+PIECES = ROW_TILES // PIECE_TILES
+PIECE_COLS = PIECE_TILES * P
+CHUNK_TILES = 4
+CHUNK_COLS = CHUNK_TILES * P
+CHUNKS = ROW_TILES // CHUNK_TILES
+
+ROUND_MAGIC = 1.5 * 2.0**23
+EXP_CAP = 2.0**60
+SCALAR_BANKS = 3
+
+
+def tile_mamba3mimoblock_pa_kernel(
+    tc, x, state_re, state_im, W_dt, b_dt, W_ph, b_ph, W_B, A_real, A_imag, out_0, out_1
+):
+    nc = tc.nc
+    with ExitStack() as ctx:
+        const = ctx.enter_context(tc.tile_pool(name="const", bufs=1))
+        xpool = ctx.enter_context(tc.tile_pool(name="xpool", bufs=6))
+        stage = ctx.enter_context(tc.tile_pool(name="stage", bufs=3))
+        keep = ctx.enter_context(tc.tile_pool(name="keep", bufs=1))
+        chan = ctx.enter_context(tc.tile_pool(name="chan", bufs=CHUNKS))
+        rows = ctx.enter_context(tc.tile_pool(name="rows", bufs=2))
+        psum = ctx.enter_context(tc.psum_pool(name="psum", bufs=8))
+        ctx.enter_context(tc.manual_schedule())
+
+        x_rows = x.rearrange("(p t) k -> p t k", t=ROW_TILES)
+        re_rows = out_0.rearrange("(p t) r -> p t r", t=ROW_TILES)
+        im_rows = out_1.rearrange("(p t) r -> p t r", t=ROW_TILES)
+
+        vec_rows = const.tile([P, P], BF16)
+        nc.vector.memset(vec_rows[:], 0.0)
+        for i, vec in enumerate((b_dt, b_ph, A_real, A_imag)):
+            nc.scalar.dma_start(out=vec_rows[i : i + 1, :], in_=vec.rearrange("(o r) -> o r", o=1))
+
+        w_sb = const.tile([P, 3, D], BF16)
+        nc.sync.dma_start(out=w_sb[:, 0, :], in_=W_dt)
+        nc.sync.dma_start(out=w_sb[:, 1, :], in_=W_ph)
+        x_sb = []
+        for piece in range(PIECES):
+            x_piece = xpool.tile([P, PIECE_TILES, D], BF16)
+            t0 = piece * PIECE_TILES
+            nc.sync.dma_start(out=x_piece[:], in_=x_rows[:, t0 : t0 + PIECE_TILES, :])
+            x_sb.append(x_piece)
+        nc.sync.dma_start(out=w_sb[:, 2, :], in_=W_B)
+        st_re = const.tile([P, ROW_TILES, R], BF16)
+        st_im = const.tile([P, ROW_TILES, R], BF16)
+        nc.sync.dma_start(out=st_re[:], in_=state_re.rearrange("(p t) r -> p t r", t=ROW_TILES))
+        nc.sync.dma_start(out=st_im[:], in_=state_im.rearrange("(p t) r -> p t r", t=ROW_TILES))
+
+        ident = const.tile([P, P], F32)
+        make_identity(nc, ident[:])
+
+        def transposes_and_copies(words, n_tiles, scalar_banks):
+            grouped = stage.tile([P, PASSES * n_tiles * P * PACK], BF16, tag="grouped", align_bytes=64)
+            grouped_words = grouped[:].bitcast(F32).rearrange("q (g c u) -> q g c u", g=PASSES, u=2)
+            for g in range(PASSES):
+                bank = psum.tile([P, 2, n_tiles, P], F32, tag="bank")
+                for u in range(2):
+                    w0 = g * WORDS_PASS + u * P
+                    for j in range(n_tiles):
+                        nc.tensor.transpose(bank[:, u, j, :], words[:, j, w0 : w0 + P], ident[:])
+                planes = bank[:].rearrange("q u j p -> q (j p) u")
+                if g < scalar_banks:
+                    nc.scalar.copy(out=grouped_words[:, g], in_=planes)
+                else:
+                    nc.vector.tensor_copy(out=grouped_words[:, g], in_=planes)
+            return grouped
+
+        w_words = w_sb[:].bitcast(F32)
+        w2_codes = keep.tile([P, PASSES, 2, P], U32, align_bytes=64)
+        w2_scales = keep.tile([P, PASSES, 2, P], U8, align_bytes=64)
+        wb_codes = keep.tile([P, PASSES, P], U32, align_bytes=64)
+        wb_scales = keep.tile([P, PASSES, P], U8, align_bytes=64)
+        w2_grouped = transposes_and_copies(w_words[:, 0:2, :], 2, 2)
+        nc.vector.quantize_mx(
+            out=w2_codes[:].rearrange("q g j r -> q (g j r)").bitcast(FP8X4),
+            scales=w2_scales[:].rearrange("q g j r -> q (g j r)"),
+            in_=w2_grouped[:],
+        )
+
+        vec_f32 = const.tile([P, P], F32)
+        nc.vector.tensor_copy(out=vec_f32[:], in_=vec_rows[:])
+        vec_t = psum.tile([P, P], F32, tag="bank")
+        nc.tensor.transpose(vec_t[:], vec_f32[:], ident[:])
+        per_chan = const.tile([P, 4], F32)
+        nc.vector.tensor_copy(out=per_chan[:], in_=vec_t[:, 0:4])
+        b_dt_col = per_chan[:, 0:1]
+        b_ph_col = per_chan[:, 1:2]
+        a_col = const.tile([P, 1], F32)
+        nc.scalar.activation(out=a_col[:], in_=per_chan[:, 2:3], func=ACT.Exp)
+        neg_a_col = const.tile([P, 1], F32)
+        nc.vector.tensor_scalar_mul(out=neg_a_col[:], in0=a_col[:], scalar1=-1.0)
+        turns_col = const.tile([P, 1], F32)
+        nc.vector.tensor_scalar_mul(out=turns_col[:], in0=per_chan[:, 3:4], scalar1=1.0 / (2.0 * math.pi))
+
+        x_codes = keep.tile([P, PIECES, PASSES, PIECE_TILES, P], U32, align_bytes=64)
+        x_scales = keep.tile([P, PIECES, PASSES, PIECE_TILES, P], U8, align_bytes=64)
+        x_grouped = {}
+        z_dt = {}
+        z_ph = {}
+        soft = {}
+        turn = {}
+        frac = {}
+        decay = {}
+        cosd = {}
+        sind = {}
+
+        def quantise(piece):
+            nc.vector.quantize_mx(
+                out=x_codes[:, piece].rearrange("q g j p -> q (g j p)").bitcast(FP8X4),
+                scales=x_scales[:, piece].rearrange("q g j p -> q (g j p)"),
+                in_=x_grouped[piece][:],
+            )
+
+        def products(piece):
+            chunk = piece // 2
+            half = piece % 2
+            if half == 0:
+                z_dt[chunk] = psum.tile([P, CHUNK_COLS], F32, name="z_dt", tag="bank")
+                z_ph[chunk] = psum.tile([P, CHUNK_COLS], F32, name="z_ph", tag="bank")
+            cols = slice(half * PIECE_COLS, (half + 1) * PIECE_COLS)
+            for i, z in enumerate((z_dt[chunk], z_ph[chunk])):
+                for g in range(PASSES):
+                    nc.tensor.matmul_mx(
+                        out=z[:, cols],
+                        lhsT=w2_codes[:, g, i, :].bitcast(FP8X4),
+                        lhsT_scale=w2_scales[:, g, i, :],
+                        rhs=x_codes[:, piece, g].rearrange("q j p -> q (j p)").bitcast(FP8X4),
+                        rhs_scale=x_scales[:, piece, g].rearrange("q j p -> q (j p)"),
+                        start=(g == 0),
+                        stop=(g == PASSES - 1),
+                    )
+
+        def first_functions(c):
+            soft[c] = chan.tile([P, CHUNK_COLS], F32, name="soft", tag="soft")
+            turn[c] = chan.tile([P, CHUNK_COLS], F32, name="turn", tag="turn")
+            nc.scalar.activation(out=soft[c][:], in_=z_dt[c][:], func=ACT.Exp, bias=b_dt_col, scale=1.0)
+            nc.scalar.activation(out=turn[c][:], in_=z_ph[c][:], func=ACT.Tanh, bias=b_ph_col, scale=1.0)
+            nc.vector.tensor_scalar_min(out=soft[c][:], in0=soft[c][:], scalar1=EXP_CAP)
+            nc.vector.tensor_scalar_mul(out=turn[c][:], in0=turn[c][:], scalar1=0.5)
+
+        def logarithm(c):
+            nc.scalar.activation(out=soft[c][:], in_=soft[c][:], func=ACT.Ln, bias=1.0, scale=1.0)
+
+        def step_and_decay(c):
+            nc.vector.scalar_tensor_tensor(
+                out=soft[c][:], in0=z_dt[c][:], scalar=b_dt_col, in1=soft[c][:], op0=ALU.add, op1=ALU.max
+            )
+            decay[c] = chan.tile([P, CHUNK_COLS], F32, name="decay", tag="decay")
+            nc.scalar.activation(out=decay[c][:], in_=soft[c][:], func=ACT.Exp, scale=neg_a_col[:])
+
+        def angle(c):
+            nc.vector.scalar_tensor_tensor(
+                out=turn[c][:], in0=soft[c][:], scalar=turns_col[:], in1=turn[c][:], op0=ALU.mult, op1=ALU.add
+            )
+            frac[c] = chan.tile([P, CHUNK_COLS], F32, name="frac", tag="frac")
+            nc.vector.tensor_scalar(
+                out=frac[c][:], in0=turn[c][:], scalar1=ROUND_MAGIC, scalar2=ROUND_MAGIC,
+                op0=ALU.add, op1=ALU.subtract,
+            )
+            nc.vector.tensor_sub(out=frac[c][:], in0=frac[c][:], in1=turn[c][:])
+
+        def trig(c):
+            cosd[c] = chan.tile([P, CHUNK_COLS], F32, name="cosd", tag="cosd")
+            sind[c] = chan.tile([P, CHUNK_COLS], F32, name="sind", tag="sind")
+            nc.scalar.activation(out=sind[c][:], in_=frac[c][:], func=ACT.Sin, scale=-2.0 * math.pi)
+            nc.scalar.activation(out=cosd[c][:], in_=frac[c][:], func=ACT.Abs)
+            nc.scalar.activation(out=cosd[c][:], in_=cosd[c][:], func=ACT.Sin, scale=-2.0 * math.pi, bias=math.pi / 2.0)
+            nc.gpsimd.tensor_mul(out=sind[c][:], in0=sind[c][:], in1=decay[c][:])
+            nc.gpsimd.tensor_mul(out=cosd[c][:], in0=cosd[c][:], in1=decay[c][:])
+
+        def row_stage(c):
+            t0 = c * CHUNK_TILES
+            z_b = psum.tile([P, CHUNK_TILES, R], F32, tag="bank")
+            for jj in range(CHUNK_TILES):
+                piece = (t0 + jj) // PIECE_TILES
+                j = (t0 + jj) % PIECE_TILES
+                for g in range(PASSES):
+                    nc.tensor.matmul_mx(
+                        out=z_b[:, jj, :],
+                        lhsT=x_codes[:, piece, g, j, :].bitcast(FP8X4),
+                        lhsT_scale=x_scales[:, piece, g, j, :],
+                        rhs=wb_codes[:, g, :].bitcast(FP8X4),
+                        rhs_scale=wb_scales[:, g, :],
+                        start=(g == 0),
+                        stop=(g == PASSES - 1),
+                    )
+            sin_t = psum.tile([P, CHUNK_TILES, R], F32, tag="bank")
+            cos_t = psum.tile([P, CHUNK_TILES, R], F32, tag="bank")
+            for jj in range(CHUNK_TILES):
+                nc.tensor.transpose(sin_t[:, jj, :], sind[c][:, jj * P : (jj + 1) * P], ident[:])
+            for jj in range(CHUNK_TILES):
+                nc.tensor.transpose(cos_t[:, jj, :], cosd[c][:, jj * P : (jj + 1) * P], ident[:])
+            sr = st_re[:, t0 : t0 + CHUNK_TILES, :]
+            si = st_im[:, t0 : t0 + CHUNK_TILES, :]
+            rc = rows.tile([P, CHUNK_TILES, R], F32, tag="rc")
+            i_s = rows.tile([P, CHUNK_TILES, R], F32, tag="i_s")
+            rs = rows.tile([P, CHUNK_TILES, R], F32, tag="rs")
+            ic = rows.tile([P, CHUNK_TILES, R], F32, tag="ic")
+            nc.vector.tensor_mul(out=rs[:], in0=sr, in1=sin_t[:])
+            nc.vector.tensor_mul(out=ic[:], in0=si, in1=cos_t[:])
+            nc.gpsimd.tensor_add(out=rs[:], in0=rs[:], in1=ic[:])
+            nc.vector.tensor_mul(out=i_s[:], in0=si, in1=sin_t[:])
+            nc.vector.tensor_mul(out=rc[:], in0=sr, in1=cos_t[:])
+            nc.vector.tensor_sub(out=rc[:], in0=rc[:], in1=i_s[:])
+            nc.vector.tensor_add(out=rc[:], in0=rc[:], in1=z_b[:])
+            nc.sync.dma_start(out=im_rows[:, t0 : t0 + CHUNK_TILES, :], in_=rs[:])
+            nc.sync.dma_start(out=re_rows[:, t0 : t0 + CHUNK_TILES, :], in_=rc[:])
+
+        def stream_step(i):
+            if 1 <= i <= PIECES:
+                quantise(i - 1)
+            if i < PIECES:
+                x_grouped[i] = transposes_and_copies(x_sb[i][:].bitcast(F32), PIECE_TILES, SCALAR_BANKS)
+            if 1 <= i <= PIECES:
+                products(i - 1)
+            if i >= 3 and i % 2 == 1:
+                first_functions((i - 3) // 2)
+
+        for i in range(0, 6):
+            stream_step(i)
+        logarithm(0)
+        logarithm(1)
+        stream_step(6)
+        step_and_decay(0)
+        step_and_decay(1)
+        stream_step(7)
+        angle(0)
+        stream_step(8)
+        angle(1)
+        stream_step(9)
+        wb_grouped = transposes_and_copies(w_words[:, 2:3, :], 1, 0)
+        nc.vector.quantize_mx(
+            out=wb_codes[:].rearrange("q g r -> q (g r)").bitcast(FP8X4),
+            scales=wb_scales[:].rearrange("q g r -> q (g r)"),
+            in_=wb_grouped[:],
+        )
+        trig(0)
+        trig(1)
+        logarithm(2)
+        logarithm(3)
+        row_stage(0)
+        step_and_decay(2)
+        step_and_decay(3)
+        angle(2)
+        angle(3)
+        row_stage(1)
+        trig(2)
+        trig(3)
+        row_stage(2)
+        row_stage(3)

@@ -28,10 +28,14 @@ PIECE_COLS = PIECE_TILES * P
 CHUNK_TILES = 4
 CHUNK_COLS = CHUNK_TILES * P
 CHUNKS = ROW_TILES // CHUNK_TILES
+PIECES_PER_CHUNK = CHUNK_TILES // PIECE_TILES
+
+X_BUFFERS = 6
+PRODUCT_LAG = 2
+PSUM_BANKS = 8
 
 ROUND_MAGIC = 1.5 * 2.0**23
 EXP_CAP = 2.0**60
-SCALAR_BANKS = 3
 
 
 def tile_mamba3mimoblock_pa_kernel(
@@ -40,12 +44,12 @@ def tile_mamba3mimoblock_pa_kernel(
     nc = tc.nc
     with ExitStack() as ctx:
         const = ctx.enter_context(tc.tile_pool(name="const", bufs=1))
-        xpool = ctx.enter_context(tc.tile_pool(name="xpool", bufs=6))
+        xpool = ctx.enter_context(tc.tile_pool(name="xpool", bufs=X_BUFFERS))
         stage = ctx.enter_context(tc.tile_pool(name="stage", bufs=3))
         keep = ctx.enter_context(tc.tile_pool(name="keep", bufs=1))
         chan = ctx.enter_context(tc.tile_pool(name="chan", bufs=CHUNKS))
-        rows = ctx.enter_context(tc.tile_pool(name="rows", bufs=2))
-        psum = ctx.enter_context(tc.psum_pool(name="psum", bufs=8))
+        rows = ctx.enter_context(tc.tile_pool(name="rows", bufs=CHUNKS))
+        psum = ctx.enter_context(tc.psum_pool(name="psum", bufs=PSUM_BANKS))
         ctx.enter_context(tc.manual_schedule())
 
         x_rows = x.rearrange("(p t) k -> p t k", t=ROW_TILES)
@@ -75,7 +79,7 @@ def tile_mamba3mimoblock_pa_kernel(
         ident = const.tile([P, P], F32)
         make_identity(nc, ident[:])
 
-        def transposes_and_copies(words, n_tiles, scalar_banks):
+        def transposes_and_copies(words, n_tiles, scalar_helps):
             grouped = stage.tile([P, PASSES * n_tiles * P * PACK], BF16, tag="grouped", align_bytes=64)
             grouped_words = grouped[:].bitcast(F32).rearrange("q (g c u) -> q g c u", g=PASSES, u=2)
             for g in range(PASSES):
@@ -84,11 +88,11 @@ def tile_mamba3mimoblock_pa_kernel(
                     w0 = g * WORDS_PASS + u * P
                     for j in range(n_tiles):
                         nc.tensor.transpose(bank[:, u, j, :], words[:, j, w0 : w0 + P], ident[:])
-                planes = bank[:].rearrange("q u j p -> q (j p) u")
-                if g < scalar_banks:
-                    nc.scalar.copy(out=grouped_words[:, g], in_=planes)
+                halves = bank[:].rearrange("q u j p -> q (j p) u")
+                if scalar_helps and g % 2 == 0:
+                    nc.scalar.copy(out=grouped_words[:, g], in_=halves)
                 else:
-                    nc.vector.tensor_copy(out=grouped_words[:, g], in_=planes)
+                    nc.vector.tensor_copy(out=grouped_words[:, g], in_=halves)
             return grouped
 
         w_words = w_sb[:].bitcast(F32)
@@ -96,7 +100,7 @@ def tile_mamba3mimoblock_pa_kernel(
         w2_scales = keep.tile([P, PASSES, 2, P], U8, align_bytes=64)
         wb_codes = keep.tile([P, PASSES, P], U32, align_bytes=64)
         wb_scales = keep.tile([P, PASSES, P], U8, align_bytes=64)
-        w2_grouped = transposes_and_copies(w_words[:, 0:2, :], 2, 2)
+        w2_grouped = transposes_and_copies(w_words[:, 0:2, :], 2, True)
         nc.vector.quantize_mx(
             out=w2_codes[:].rearrange("q g j r -> q (g j r)").bitcast(FP8X4),
             scales=w2_scales[:].rearrange("q g j r -> q (g j r)"),
@@ -120,31 +124,32 @@ def tile_mamba3mimoblock_pa_kernel(
 
         x_codes = keep.tile([P, PIECES, PASSES, PIECE_TILES, P], U32, align_bytes=64)
         x_scales = keep.tile([P, PIECES, PASSES, PIECE_TILES, P], U8, align_bytes=64)
-        x_grouped = {}
         z_dt = {}
         z_ph = {}
+        z_b = {}
         soft = {}
         turn = {}
         frac = {}
-        decay = {}
-        cosd = {}
-        sind = {}
+        sine = {}
+        cosine = {}
+        re_part = {}
+        im_part = {}
 
-        def quantise(piece):
+        def quantise(piece, grouped):
             nc.vector.quantize_mx(
                 out=x_codes[:, piece].rearrange("q g j p -> q (g j p)").bitcast(FP8X4),
                 scales=x_scales[:, piece].rearrange("q g j p -> q (g j p)"),
-                in_=x_grouped[piece][:],
+                in_=grouped[:],
             )
 
         def products(piece):
-            chunk = piece // 2
-            half = piece % 2
+            c = piece // PIECES_PER_CHUNK
+            half = piece % PIECES_PER_CHUNK
             if half == 0:
-                z_dt[chunk] = psum.tile([P, CHUNK_COLS], F32, name="z_dt", tag="bank")
-                z_ph[chunk] = psum.tile([P, CHUNK_COLS], F32, name="z_ph", tag="bank")
+                z_dt[c] = psum.tile([P, CHUNK_COLS], F32, name="z_dt", tag="bank")
+                z_ph[c] = psum.tile([P, CHUNK_COLS], F32, name="z_ph", tag="bank")
             cols = slice(half * PIECE_COLS, (half + 1) * PIECE_COLS)
-            for i, z in enumerate((z_dt[chunk], z_ph[chunk])):
+            for i, z in enumerate((z_dt[c], z_ph[c])):
                 for g in range(PASSES):
                     nc.tensor.matmul_mx(
                         out=z[:, cols],
@@ -156,53 +161,26 @@ def tile_mamba3mimoblock_pa_kernel(
                         stop=(g == PASSES - 1),
                     )
 
-        def first_functions(c):
+        def exp_and_tanh(c):
             soft[c] = chan.tile([P, CHUNK_COLS], F32, name="soft", tag="soft")
             turn[c] = chan.tile([P, CHUNK_COLS], F32, name="turn", tag="turn")
             nc.scalar.activation(out=soft[c][:], in_=z_dt[c][:], func=ACT.Exp, bias=b_dt_col, scale=1.0)
             nc.scalar.activation(out=turn[c][:], in_=z_ph[c][:], func=ACT.Tanh, bias=b_ph_col, scale=1.0)
-            nc.vector.tensor_scalar_min(out=soft[c][:], in0=soft[c][:], scalar1=EXP_CAP)
-            nc.vector.tensor_scalar_mul(out=turn[c][:], in0=turn[c][:], scalar1=0.5)
-
-        def logarithm(c):
-            nc.scalar.activation(out=soft[c][:], in_=soft[c][:], func=ACT.Ln, bias=1.0, scale=1.0)
-
-        def step_and_decay(c):
-            nc.vector.scalar_tensor_tensor(
-                out=soft[c][:], in0=z_dt[c][:], scalar=b_dt_col, in1=soft[c][:], op0=ALU.add, op1=ALU.max
+            nc.gpsimd.tensor_scalar(
+                out=soft[c][:], in0=soft[c][:], scalar1=EXP_CAP, scalar2=0.0, op0=ALU.min, op1=ALU.add
             )
-            decay[c] = chan.tile([P, CHUNK_COLS], F32, name="decay", tag="decay")
-            nc.scalar.activation(out=decay[c][:], in_=soft[c][:], func=ACT.Exp, scale=neg_a_col[:])
-
-        def angle(c):
-            nc.vector.scalar_tensor_tensor(
-                out=turn[c][:], in0=soft[c][:], scalar=turns_col[:], in1=turn[c][:], op0=ALU.mult, op1=ALU.add
+            nc.gpsimd.tensor_scalar(
+                out=turn[c][:], in0=turn[c][:], scalar1=0.5, scalar2=0.0, op0=ALU.mult, op1=ALU.add
             )
-            frac[c] = chan.tile([P, CHUNK_COLS], F32, name="frac", tag="frac")
-            nc.vector.tensor_scalar(
-                out=frac[c][:], in0=turn[c][:], scalar1=ROUND_MAGIC, scalar2=ROUND_MAGIC,
-                op0=ALU.add, op1=ALU.subtract,
-            )
-            nc.vector.tensor_sub(out=frac[c][:], in0=frac[c][:], in1=turn[c][:])
 
-        def trig(c):
-            cosd[c] = chan.tile([P, CHUNK_COLS], F32, name="cosd", tag="cosd")
-            sind[c] = chan.tile([P, CHUNK_COLS], F32, name="sind", tag="sind")
-            nc.scalar.activation(out=sind[c][:], in_=frac[c][:], func=ACT.Sin, scale=-2.0 * math.pi)
-            nc.scalar.activation(out=cosd[c][:], in_=frac[c][:], func=ACT.Abs)
-            nc.scalar.activation(out=cosd[c][:], in_=cosd[c][:], func=ACT.Sin, scale=-2.0 * math.pi, bias=math.pi / 2.0)
-            nc.gpsimd.tensor_mul(out=sind[c][:], in0=sind[c][:], in1=decay[c][:])
-            nc.gpsimd.tensor_mul(out=cosd[c][:], in0=cosd[c][:], in1=decay[c][:])
-
-        def row_stage(c):
-            t0 = c * CHUNK_TILES
-            z_b = psum.tile([P, CHUNK_TILES, R], F32, tag="bank")
+        def b_val(c):
+            z_b[c] = psum.tile([P, CHUNK_TILES, R], F32, name="z_b", tag="bank")
             for jj in range(CHUNK_TILES):
-                piece = (t0 + jj) // PIECE_TILES
-                j = (t0 + jj) % PIECE_TILES
+                piece = (c * CHUNK_TILES + jj) // PIECE_TILES
+                j = (c * CHUNK_TILES + jj) % PIECE_TILES
                 for g in range(PASSES):
                     nc.tensor.matmul_mx(
-                        out=z_b[:, jj, :],
+                        out=z_b[c][:, jj, :],
                         lhsT=x_codes[:, piece, g, j, :].bitcast(FP8X4),
                         lhsT_scale=x_scales[:, piece, g, j, :],
                         rhs=wb_codes[:, g, :].bitcast(FP8X4),
@@ -210,67 +188,97 @@ def tile_mamba3mimoblock_pa_kernel(
                         start=(g == 0),
                         stop=(g == PASSES - 1),
                     )
-            sin_t = psum.tile([P, CHUNK_TILES, R], F32, tag="bank")
-            cos_t = psum.tile([P, CHUNK_TILES, R], F32, tag="bank")
+
+        def logarithm(c):
+            nc.scalar.activation(out=soft[c][:], in_=soft[c][:], func=ACT.Ln, bias=1.0, scale=1.0)
+
+        def step_and_angle(c):
+            nc.vector.scalar_tensor_tensor(
+                out=soft[c][:], in0=z_dt[c][:], scalar=b_dt_col, in1=soft[c][:], op0=ALU.add, op1=ALU.max
+            )
+            nc.vector.scalar_tensor_tensor(
+                out=turn[c][:], in0=soft[c][:], scalar=turns_col[:], in1=turn[c][:], op0=ALU.mult, op1=ALU.add
+            )
+            frac[c] = chan.tile([P, CHUNK_COLS], F32, name="frac", tag="frac")
+            nc.gpsimd.tensor_scalar(
+                out=frac[c][:], in0=turn[c][:], scalar1=ROUND_MAGIC, scalar2=ROUND_MAGIC,
+                op0=ALU.add, op1=ALU.subtract,
+            )
+            nc.gpsimd.tensor_sub(out=frac[c][:], in0=frac[c][:], in1=turn[c][:])
+
+        def sine_and_cosine(c):
+            sine[c] = chan.tile([P, CHUNK_COLS], F32, name="sine", tag="sine")
+            cosine[c] = chan.tile([P, CHUNK_COLS], F32, name="cosine", tag="cosine")
+            nc.scalar.activation(out=sine[c][:], in_=frac[c][:], func=ACT.Sin, scale=-2.0 * math.pi)
+            nc.scalar.activation(out=cosine[c][:], in_=frac[c][:], func=ACT.Abs)
+            nc.scalar.activation(
+                out=cosine[c][:], in_=cosine[c][:], func=ACT.Sin, scale=-2.0 * math.pi, bias=math.pi / 2.0
+            )
+
+        def decay(c):
+            nc.scalar.activation(out=soft[c][:], in_=soft[c][:], func=ACT.Exp, scale=neg_a_col[:])
+
+        def back_to_rows(channel_tile):
+            bank = psum.tile([P, CHUNK_TILES, R], F32, name="row_bank", tag="bank")
             for jj in range(CHUNK_TILES):
-                nc.tensor.transpose(sin_t[:, jj, :], sind[c][:, jj * P : (jj + 1) * P], ident[:])
-            for jj in range(CHUNK_TILES):
-                nc.tensor.transpose(cos_t[:, jj, :], cosd[c][:, jj * P : (jj + 1) * P], ident[:])
+                nc.tensor.transpose(bank[:, jj, :], channel_tile[:, jj * P : (jj + 1) * P], ident[:])
+            return bank
+
+        def rotate(c):
+            t0 = c * CHUNK_TILES
             sr = st_re[:, t0 : t0 + CHUNK_TILES, :]
             si = st_im[:, t0 : t0 + CHUNK_TILES, :]
-            rc = rows.tile([P, CHUNK_TILES, R], F32, tag="rc")
-            i_s = rows.tile([P, CHUNK_TILES, R], F32, tag="i_s")
-            rs = rows.tile([P, CHUNK_TILES, R], F32, tag="rs")
-            ic = rows.tile([P, CHUNK_TILES, R], F32, tag="ic")
-            nc.vector.tensor_mul(out=rs[:], in0=sr, in1=sin_t[:])
-            nc.vector.tensor_mul(out=ic[:], in0=si, in1=cos_t[:])
-            nc.gpsimd.tensor_add(out=rs[:], in0=rs[:], in1=ic[:])
-            nc.vector.tensor_mul(out=i_s[:], in0=si, in1=sin_t[:])
-            nc.vector.tensor_mul(out=rc[:], in0=sr, in1=cos_t[:])
-            nc.vector.tensor_sub(out=rc[:], in0=rc[:], in1=i_s[:])
-            nc.vector.tensor_add(out=rc[:], in0=rc[:], in1=z_b[:])
-            nc.sync.dma_start(out=im_rows[:, t0 : t0 + CHUNK_TILES, :], in_=rs[:])
-            nc.sync.dma_start(out=re_rows[:, t0 : t0 + CHUNK_TILES, :], in_=rc[:])
+            sin_t = back_to_rows(sine[c])
+            cos_t = back_to_rows(cosine[c])
+            re_sin = rows.tile([P, CHUNK_TILES, R], F32, tag="re_sin")
+            im_sin = rows.tile([P, CHUNK_TILES, R], F32, tag="im_sin")
+            re_cos = rows.tile([P, CHUNK_TILES, R], F32, tag="re_cos")
+            im_cos = rows.tile([P, CHUNK_TILES, R], F32, tag="im_cos")
+            nc.vector.tensor_mul(out=re_sin[:], in0=sr, in1=sin_t[:])
+            nc.vector.tensor_mul(out=im_sin[:], in0=si, in1=sin_t[:])
+            nc.vector.tensor_mul(out=re_cos[:], in0=sr, in1=cos_t[:])
+            nc.vector.tensor_mul(out=im_cos[:], in0=si, in1=cos_t[:])
+            nc.gpsimd.tensor_add(out=re_sin[:], in0=re_sin[:], in1=im_cos[:])
+            nc.gpsimd.tensor_sub(out=re_cos[:], in0=re_cos[:], in1=im_sin[:])
+            im_part[c] = re_sin
+            re_part[c] = re_cos
 
-        def stream_step(i):
-            if 1 <= i <= PIECES:
-                quantise(i - 1)
-            if i < PIECES:
-                x_grouped[i] = transposes_and_copies(x_sb[i][:].bitcast(F32), PIECE_TILES, SCALAR_BANKS)
-            if 1 <= i <= PIECES:
-                products(i - 1)
-            if i >= 3 and i % 2 == 1:
-                first_functions((i - 3) // 2)
+        def damp_and_store(c):
+            t0 = c * CHUNK_TILES
+            decay_t = back_to_rows(soft[c])
+            nc.vector.tensor_mul(out=im_part[c][:], in0=im_part[c][:], in1=decay_t[:])
+            nc.sync.dma_start(out=im_rows[:, t0 : t0 + CHUNK_TILES, :], in_=im_part[c][:])
+            nc.vector.tensor_mul(out=re_part[c][:], in0=re_part[c][:], in1=decay_t[:])
+            nc.vector.tensor_add(out=re_part[c][:], in0=re_part[c][:], in1=z_b[c][:])
+            nc.sync.dma_start(out=re_rows[:, t0 : t0 + CHUNK_TILES, :], in_=re_part[c][:])
 
-        for i in range(0, 6):
-            stream_step(i)
-        logarithm(0)
-        logarithm(1)
-        stream_step(6)
-        step_and_decay(0)
-        step_and_decay(1)
-        stream_step(7)
-        angle(0)
-        stream_step(8)
-        angle(1)
-        stream_step(9)
-        wb_grouped = transposes_and_copies(w_words[:, 2:3, :], 1, 0)
+        for step in range(PIECES + PRODUCT_LAG):
+            if step < PIECES:
+                quantise(step, transposes_and_copies(x_sb[step][:].bitcast(F32), PIECE_TILES, True))
+            piece = step - PRODUCT_LAG
+            if piece >= 0:
+                products(piece)
+                if piece % PIECES_PER_CHUNK == PIECES_PER_CHUNK - 1:
+                    exp_and_tanh(piece // PIECES_PER_CHUNK)
+
+        wb_grouped = transposes_and_copies(w_words[:, 2:3, :], 1, False)
         nc.vector.quantize_mx(
             out=wb_codes[:].rearrange("q g r -> q (g r)").bitcast(FP8X4),
             scales=wb_scales[:].rearrange("q g r -> q (g r)"),
             in_=wb_grouped[:],
         )
-        trig(0)
-        trig(1)
-        logarithm(2)
-        logarithm(3)
-        row_stage(0)
-        step_and_decay(2)
-        step_and_decay(3)
-        angle(2)
-        angle(3)
-        row_stage(1)
-        trig(2)
-        trig(3)
-        row_stage(2)
-        row_stage(3)
+        for c in range(CHUNKS):
+            b_val(c)
+
+        for c in range(CHUNKS):
+            logarithm(c)
+        for c in range(CHUNKS):
+            step_and_angle(c)
+        for c in range(CHUNKS):
+            sine_and_cosine(c)
+        for c in range(CHUNKS):
+            decay(c)
+        for c in range(CHUNKS):
+            rotate(c)
+        for c in range(CHUNKS):
+            damp_and_store(c)

@@ -33,6 +33,7 @@ PIECES_PER_CHUNK = CHUNK_TILES // PIECE_TILES
 X_BUFFERS = 6
 PRODUCT_LAG = 2
 PSUM_BANKS = 8
+SCALAR_BANKS = 3
 
 ROUND_MAGIC = 1.5 * 2.0**23
 EXP_CAP = 2.0**60
@@ -79,7 +80,7 @@ def tile_mamba3mimoblock_pa_kernel(
         ident = const.tile([P, P], F32)
         make_identity(nc, ident[:])
 
-        def transposes_and_copies(words, n_tiles, scalar_helps):
+        def transposes_and_copies(words, n_tiles, scalar_banks):
             grouped = stage.tile([P, PASSES * n_tiles * P * PACK], BF16, tag="grouped", align_bytes=64)
             grouped_words = grouped[:].bitcast(F32).rearrange("q (g c u) -> q g c u", g=PASSES, u=2)
             for g in range(PASSES):
@@ -89,7 +90,7 @@ def tile_mamba3mimoblock_pa_kernel(
                     for j in range(n_tiles):
                         nc.tensor.transpose(bank[:, u, j, :], words[:, j, w0 : w0 + P], ident[:])
                 halves = bank[:].rearrange("q u j p -> q (j p) u")
-                if scalar_helps and g % 2 == 0:
+                if g < scalar_banks:
                     nc.scalar.copy(out=grouped_words[:, g], in_=halves)
                 else:
                     nc.vector.tensor_copy(out=grouped_words[:, g], in_=halves)
@@ -100,7 +101,7 @@ def tile_mamba3mimoblock_pa_kernel(
         w2_scales = keep.tile([P, PASSES, 2, P], U8, align_bytes=64)
         wb_codes = keep.tile([P, PASSES, P], U32, align_bytes=64)
         wb_scales = keep.tile([P, PASSES, P], U8, align_bytes=64)
-        w2_grouped = transposes_and_copies(w_words[:, 0:2, :], 2, True)
+        w2_grouped = transposes_and_copies(w_words[:, 0:2, :], 2, 2)
         nc.vector.quantize_mx(
             out=w2_codes[:].rearrange("q g j r -> q (g j r)").bitcast(FP8X4),
             scales=w2_scales[:].rearrange("q g j r -> q (g j r)"),
@@ -166,12 +167,8 @@ def tile_mamba3mimoblock_pa_kernel(
             turn[c] = chan.tile([P, CHUNK_COLS], F32, name="turn", tag="turn")
             nc.scalar.activation(out=soft[c][:], in_=z_dt[c][:], func=ACT.Exp, bias=b_dt_col, scale=1.0)
             nc.scalar.activation(out=turn[c][:], in_=z_ph[c][:], func=ACT.Tanh, bias=b_ph_col, scale=1.0)
-            nc.gpsimd.tensor_scalar(
-                out=soft[c][:], in0=soft[c][:], scalar1=EXP_CAP, scalar2=0.0, op0=ALU.min, op1=ALU.add
-            )
-            nc.gpsimd.tensor_scalar(
-                out=turn[c][:], in0=turn[c][:], scalar1=0.5, scalar2=0.0, op0=ALU.mult, op1=ALU.add
-            )
+            nc.vector.tensor_scalar_min(out=soft[c][:], in0=soft[c][:], scalar1=EXP_CAP)
+            nc.vector.tensor_scalar_mul(out=turn[c][:], in0=turn[c][:], scalar1=0.5)
 
         def b_val(c):
             z_b[c] = psum.tile([P, CHUNK_TILES, R], F32, name="z_b", tag="bank")
@@ -200,11 +197,11 @@ def tile_mamba3mimoblock_pa_kernel(
                 out=turn[c][:], in0=soft[c][:], scalar=turns_col[:], in1=turn[c][:], op0=ALU.mult, op1=ALU.add
             )
             frac[c] = chan.tile([P, CHUNK_COLS], F32, name="frac", tag="frac")
-            nc.gpsimd.tensor_scalar(
+            nc.vector.tensor_scalar(
                 out=frac[c][:], in0=turn[c][:], scalar1=ROUND_MAGIC, scalar2=ROUND_MAGIC,
                 op0=ALU.add, op1=ALU.subtract,
             )
-            nc.gpsimd.tensor_sub(out=frac[c][:], in0=frac[c][:], in1=turn[c][:])
+            nc.vector.tensor_sub(out=frac[c][:], in0=frac[c][:], in1=turn[c][:])
 
         def sine_and_cosine(c):
             sine[c] = chan.tile([P, CHUNK_COLS], F32, name="sine", tag="sine")
@@ -254,14 +251,14 @@ def tile_mamba3mimoblock_pa_kernel(
 
         for step in range(PIECES + PRODUCT_LAG):
             if step < PIECES:
-                quantise(step, transposes_and_copies(x_sb[step][:].bitcast(F32), PIECE_TILES, True))
+                quantise(step, transposes_and_copies(x_sb[step][:].bitcast(F32), PIECE_TILES, SCALAR_BANKS))
             piece = step - PRODUCT_LAG
             if piece >= 0:
                 products(piece)
                 if piece % PIECES_PER_CHUNK == PIECES_PER_CHUNK - 1:
                     exp_and_tanh(piece // PIECES_PER_CHUNK)
 
-        wb_grouped = transposes_and_copies(w_words[:, 2:3, :], 1, False)
+        wb_grouped = transposes_and_copies(w_words[:, 2:3, :], 1, 0)
         nc.vector.quantize_mx(
             out=wb_codes[:].rearrange("q g r -> q (g r)").bitcast(FP8X4),
             scales=wb_scales[:].rearrange("q g r -> q (g r)"),

@@ -33,6 +33,7 @@ PIECES_PER_CHUNK = CHUNK_TILES // PIECE_TILES
 X_BUFFERS = 6
 PRODUCT_LAG = 2
 PSUM_BANKS = 8
+ABREAST = 2
 SCALAR_BANKS = 3
 
 ROUND_MAGIC = 1.5 * 2.0**23
@@ -189,25 +190,35 @@ def tile_mamba3mimoblock_pa_kernel(
         def logarithm(c):
             nc.scalar.activation(out=soft[c][:], in_=soft[c][:], func=ACT.Ln, bias=1.0, scale=1.0)
 
-        def step_and_angle(c):
+        def step_size(c):
             nc.vector.scalar_tensor_tensor(
                 out=soft[c][:], in0=z_dt[c][:], scalar=b_dt_col, in1=soft[c][:], op0=ALU.add, op1=ALU.max
             )
+
+        def angle_in_turns(c):
             nc.vector.scalar_tensor_tensor(
                 out=turn[c][:], in0=soft[c][:], scalar=turns_col[:], in1=turn[c][:], op0=ALU.mult, op1=ALU.add
             )
+
+        def nearest_turn(c):
             frac[c] = chan.tile([P, CHUNK_COLS], F32, name="frac", tag="frac")
             nc.vector.tensor_scalar(
                 out=frac[c][:], in0=turn[c][:], scalar1=ROUND_MAGIC, scalar2=ROUND_MAGIC,
                 op0=ALU.add, op1=ALU.subtract,
             )
+
+        def fraction(c):
             nc.vector.tensor_sub(out=frac[c][:], in0=frac[c][:], in1=turn[c][:])
 
-        def sine_and_cosine(c):
+        def sine_of(c):
             sine[c] = chan.tile([P, CHUNK_COLS], F32, name="sine", tag="sine")
-            cosine[c] = chan.tile([P, CHUNK_COLS], F32, name="cosine", tag="cosine")
             nc.scalar.activation(out=sine[c][:], in_=frac[c][:], func=ACT.Sin, scale=-2.0 * math.pi)
+
+        def magnitude_of(c):
+            cosine[c] = chan.tile([P, CHUNK_COLS], F32, name="cosine", tag="cosine")
             nc.scalar.activation(out=cosine[c][:], in_=frac[c][:], func=ACT.Abs)
+
+        def cosine_of(c):
             nc.scalar.activation(
                 out=cosine[c][:], in_=cosine[c][:], func=ACT.Sin, scale=-2.0 * math.pi, bias=math.pi / 2.0
             )
@@ -243,9 +254,9 @@ def tile_mamba3mimoblock_pa_kernel(
         def damp_and_store(c):
             t0 = c * CHUNK_TILES
             decay_t = back_to_rows(soft[c])
+            nc.vector.tensor_mul(out=re_part[c][:], in0=re_part[c][:], in1=decay_t[:])
             nc.vector.tensor_mul(out=im_part[c][:], in0=im_part[c][:], in1=decay_t[:])
             nc.sync.dma_start(out=im_rows[:, t0 : t0 + CHUNK_TILES, :], in_=im_part[c][:])
-            nc.vector.tensor_mul(out=re_part[c][:], in0=re_part[c][:], in1=decay_t[:])
             nc.vector.tensor_add(out=re_part[c][:], in0=re_part[c][:], in1=z_b[c][:])
             nc.sync.dma_start(out=re_rows[:, t0 : t0 + CHUNK_TILES, :], in_=re_part[c][:])
 
@@ -269,10 +280,24 @@ def tile_mamba3mimoblock_pa_kernel(
 
         for c in range(CHUNKS):
             logarithm(c)
-        for c in range(CHUNKS):
-            step_and_angle(c)
-        for c in range(CHUNKS):
-            sine_and_cosine(c)
+        for first in range(0, CHUNKS, ABREAST):
+            abreast = range(first, first + ABREAST)
+            for c in abreast:
+                step_size(c)
+            for c in abreast:
+                angle_in_turns(c)
+            for c in abreast:
+                nearest_turn(c)
+            for c in abreast:
+                fraction(c)
+        for first in range(0, CHUNKS, ABREAST):
+            abreast = range(first, first + ABREAST)
+            for c in abreast:
+                sine_of(c)
+            for c in abreast:
+                magnitude_of(c)
+            for c in abreast:
+                cosine_of(c)
         for c in range(CHUNKS):
             decay(c)
         for c in range(CHUNKS):

@@ -208,7 +208,7 @@ def tile_mamba3mimoblock_pa_kernel(
             )
 
         def fraction(c):
-            nc.vector.tensor_sub(out=frac[c][:], in0=frac[c][:], in1=turn[c][:])
+            nc.gpsimd.tensor_sub(out=frac[c][:], in0=frac[c][:], in1=turn[c][:])
 
         def sine_of(c):
             sine[c] = chan.tile([P, CHUNK_COLS], F32, name="sine", tag="sine")

@@ -208,7 +208,7 @@ def tile_mamba3mimoblock_pa_kernel(
             )
 
         def fraction(c):
-            nc.gpsimd.tensor_sub(out=frac[c][:], in0=frac[c][:], in1=turn[c][:])
+            nc.vector.tensor_sub(out=frac[c][:], in0=frac[c][:], in1=turn[c][:])
 
         def sine_of(c):
             sine[c] = chan.tile([P, CHUNK_COLS], F32, name="sine", tag="sine")
@@ -260,28 +260,7 @@ def tile_mamba3mimoblock_pa_kernel(
             nc.vector.tensor_add(out=re_part[c][:], in0=re_part[c][:], in1=z_b[c][:])
             nc.sync.dma_start(out=re_rows[:, t0 : t0 + CHUNK_TILES, :], in_=re_part[c][:])
 
-        for step in range(PIECES + PRODUCT_LAG):
-            if step < PIECES:
-                quantise(step, transposes_and_copies(x_sb[step][:].bitcast(F32), PIECE_TILES, SCALAR_BANKS))
-            piece = step - PRODUCT_LAG
-            if piece >= 0:
-                products(piece)
-                if piece % PIECES_PER_CHUNK == PIECES_PER_CHUNK - 1:
-                    exp_and_tanh(piece // PIECES_PER_CHUNK)
-
-        wb_grouped = transposes_and_copies(w_words[:, 2:3, :], 1, 0)
-        nc.vector.quantize_mx(
-            out=wb_codes[:].rearrange("q g r -> q (g r)").bitcast(FP8X4),
-            scales=wb_scales[:].rearrange("q g r -> q (g r)"),
-            in_=wb_grouped[:],
-        )
-        for c in range(CHUNKS):
-            b_val(c)
-
-        for c in range(CHUNKS):
-            logarithm(c)
-        for first in range(0, CHUNKS, ABREAST):
-            abreast = range(first, first + ABREAST)
+        def angles(abreast):
             for c in abreast:
                 step_size(c)
             for c in abreast:
@@ -290,6 +269,37 @@ def tile_mamba3mimoblock_pa_kernel(
                 nearest_turn(c)
             for c in abreast:
                 fraction(c)
+
+        first_half = range(0, CHUNKS // 2)
+        second_half = range(CHUNKS // 2, CHUNKS)
+
+        for piece in range(PIECES):
+            quantise(piece, transposes_and_copies(x_sb[piece][:].bitcast(F32), PIECE_TILES, SCALAR_BANKS))
+            behind = piece - PRODUCT_LAG
+            if 0 <= behind < PIECES // 2:
+                products(behind)
+                if behind % PIECES_PER_CHUNK == PIECES_PER_CHUNK - 1:
+                    exp_and_tanh(behind // PIECES_PER_CHUNK)
+
+        for c in first_half:
+            logarithm(c)
+        wb_grouped = transposes_and_copies(w_words[:, 2:3, :], 1, 0)
+        nc.vector.quantize_mx(
+            out=wb_codes[:].rearrange("q g r -> q (g r)").bitcast(FP8X4),
+            scales=wb_scales[:].rearrange("q g r -> q (g r)"),
+            in_=wb_grouped[:],
+        )
+        for piece in range(PIECES // 2, PIECES):
+            products(piece)
+        angles(first_half)
+        for c in second_half:
+            exp_and_tanh(c)
+        for c in range(CHUNKS):
+            b_val(c)
+        for c in second_half:
+            logarithm(c)
+        angles(second_half)
+
         for first in range(0, CHUNKS, ABREAST):
             abreast = range(first, first + ABREAST)
             for c in abreast:

import math
from contextlib import ExitStack

import concourse.mybir as mybir
from concourse.masks import make_identity

F32 = mybir.dt.float32
BF16 = mybir.dt.bfloat16
U32 = mybir.dt.uint32
U8 = mybir.dt.uint8
FP8X4 = mybir.dt.float8_e4m3fn_x4
ACT = mybir.ActivationFunctionType
ALU = mybir.AluOpType

B, D, R = 2048, 2048, 128
FLOPS = 2 * B * D * 3 * R

P = 128
PACK = 4
K_PASS = P * PACK
PASSES = D // K_PASS
WORDS_PASS = K_PASS // 2

ROW_TILES = B // P
PIECE_TILES = 2
PIECES = ROW_TILES // PIECE_TILES
PIECE_COLS = PIECE_TILES * P
CHUNK_TILES = 4
CHUNK_COLS = CHUNK_TILES * P
CHUNKS = ROW_TILES // CHUNK_TILES
PIECES_PER_CHUNK = CHUNK_TILES // PIECE_TILES

X_BUFFERS = 6
PRODUCT_LAG = 2
PSUM_BANKS = 8
ABREAST = 2
SCALAR_BANKS = 3

ROUND_MAGIC = 1.5 * 2.0**23
EXP_CAP = 2.0**60


def tile_mamba3mimoblock_pa_kernel(
    tc, x, state_re, state_im, W_dt, b_dt, W_ph, b_ph, W_B, A_real, A_imag, out_0, out_1
):
    nc = tc.nc
    with ExitStack() as ctx:
        const = ctx.enter_context(tc.tile_pool(name="const", bufs=1))
        xpool = ctx.enter_context(tc.tile_pool(name="xpool", bufs=X_BUFFERS))
        stage = ctx.enter_context(tc.tile_pool(name="stage", bufs=3))
        keep = ctx.enter_context(tc.tile_pool(name="keep", bufs=1))
        chan = ctx.enter_context(tc.tile_pool(name="chan", bufs=CHUNKS))
        rows = ctx.enter_context(tc.tile_pool(name="rows", bufs=CHUNKS))
        psum = ctx.enter_context(tc.psum_pool(name="psum", bufs=PSUM_BANKS))
        ctx.enter_context(tc.manual_schedule())

        x_rows = x.rearrange("(p t) k -> p t k", t=ROW_TILES)
        re_rows = out_0.rearrange("(p t) r -> p t r", t=ROW_TILES)
        im_rows = out_1.rearrange("(p t) r -> p t r", t=ROW_TILES)

        vec_rows = const.tile([P, P], BF16)
        nc.vector.memset(vec_rows[:], 0.0)
        for i, vec in enumerate((b_dt, b_ph, A_real, A_imag)):
            nc.scalar.dma_start(out=vec_rows[i : i + 1, :], in_=vec.rearrange("(o r) -> o r", o=1))

        w_sb = const.tile([P, 3, D], BF16)
        nc.sync.dma_start(out=w_sb[:, 0, :], in_=W_dt)
        nc.sync.dma_start(out=w_sb[:, 1, :], in_=W_ph)
        x_sb = []
        for piece in range(PIECES):
            x_piece = xpool.tile([P, PIECE_TILES, D], BF16)
            t0 = piece * PIECE_TILES
            nc.sync.dma_start(out=x_piece[:], in_=x_rows[:, t0 : t0 + PIECE_TILES, :])
            x_sb.append(x_piece)
        nc.sync.dma_start(out=w_sb[:, 2, :], in_=W_B)
        st_re = const.tile([P, ROW_TILES, R], BF16)
        st_im = const.tile([P, ROW_TILES, R], BF16)
        nc.sync.dma_start(out=st_re[:], in_=state_re.rearrange("(p t) r -> p t r", t=ROW_TILES))
        nc.sync.dma_start(out=st_im[:], in_=state_im.rearrange("(p t) r -> p t r", t=ROW_TILES))

        ident = const.tile([P, P], F32)
        make_identity(nc, ident[:])

        def transposes_and_copies(words, n_tiles, scalar_banks):
            grouped = stage.tile([P, PASSES * n_tiles * P * PACK], BF16, tag="grouped", align_bytes=64)
            grouped_words = grouped[:].bitcast(F32).rearrange("q (g c u) -> q g c u", g=PASSES, u=2)
            for g in range(PASSES):
                bank = psum.tile([P, 2, n_tiles, P], F32, tag="bank")
                for u in range(2):
                    w0 = g * WORDS_PASS + u * P
                    for j in range(n_tiles):
                        nc.tensor.transpose(bank[:, u, j, :], words[:, j, w0 : w0 + P], ident[:])
                halves = bank[:].rearrange("q u j p -> q (j p) u")
                if g < scalar_banks:
                    nc.scalar.copy(out=grouped_words[:, g], in_=halves)
                else:
                    nc.vector.tensor_copy(out=grouped_words[:, g], in_=halves)
            return grouped

        w_words = w_sb[:].bitcast(F32)
        w2_codes = keep.tile([P, PASSES, 2, P], U32, align_bytes=64)
        w2_scales = keep.tile([P, PASSES, 2, P], U8, align_bytes=64)
        wb_codes = keep.tile([P, PASSES, P], U32, align_bytes=64)
        wb_scales = keep.tile([P, PASSES, P], U8, align_bytes=64)
        w2_grouped = transposes_and_copies(w_words[:, 0:2, :], 2, 2)
        nc.vector.quantize_mx(
            out=w2_codes[:].rearrange("q g j r -> q (g j r)").bitcast(FP8X4),
            scales=w2_scales[:].rearrange("q g j r -> q (g j r)"),
            in_=w2_grouped[:],
        )

        vec_f32 = const.tile([P, P], F32)
        nc.vector.tensor_copy(out=vec_f32[:], in_=vec_rows[:])
        vec_t = psum.tile([P, P], F32, tag="bank")
        nc.tensor.transpose(vec_t[:], vec_f32[:], ident[:])
        per_chan = const.tile([P, 4], F32)
        nc.vector.tensor_copy(out=per_chan[:], in_=vec_t[:, 0:4])
        b_dt_col = per_chan[:, 0:1]
        b_ph_col = per_chan[:, 1:2]
        a_col = const.tile([P, 1], F32)
        nc.scalar.activation(out=a_col[:], in_=per_chan[:, 2:3], func=ACT.Exp)
        neg_a_col = const.tile([P, 1], F32)
        nc.vector.tensor_scalar_mul(out=neg_a_col[:], in0=a_col[:], scalar1=-1.0)
        turns_col = const.tile([P, 1], F32)
        nc.vector.tensor_scalar_mul(out=turns_col[:], in0=per_chan[:, 3:4], scalar1=1.0 / (2.0 * math.pi))

        x_codes = keep.tile([P, PIECES, PASSES, PIECE_TILES, P], U32, align_bytes=64)
        x_scales = keep.tile([P, PIECES, PASSES, PIECE_TILES, P], U8, align_bytes=64)
        z_dt = {}
        z_ph = {}
        z_b = {}
        soft = {}
        turn = {}
        frac = {}
        sine = {}
        cosine = {}
        re_part = {}
        im_part = {}

        def quantise(piece, grouped):
            nc.vector.quantize_mx(
                out=x_codes[:, piece].rearrange("q g j p -> q (g j p)").bitcast(FP8X4),
                scales=x_scales[:, piece].rearrange("q g j p -> q (g j p)"),
                in_=grouped[:],
            )

        def products(piece):
            c = piece // PIECES_PER_CHUNK
            half = piece % PIECES_PER_CHUNK
            if half == 0:
                z_dt[c] = psum.tile([P, CHUNK_COLS], F32, name="z_dt", tag="bank")
                z_ph[c] = psum.tile([P, CHUNK_COLS], F32, name="z_ph", tag="bank")
            cols = slice(half * PIECE_COLS, (half + 1) * PIECE_COLS)
            for i, z in enumerate((z_dt[c], z_ph[c])):
                for g in range(PASSES):
                    nc.tensor.matmul_mx(
                        out=z[:, cols],
                        lhsT=w2_codes[:, g, i, :].bitcast(FP8X4),
                        lhsT_scale=w2_scales[:, g, i, :],
                        rhs=x_codes[:, piece, g].rearrange("q j p -> q (j p)").bitcast(FP8X4),
                        rhs_scale=x_scales[:, piece, g].rearrange("q j p -> q (j p)"),
                        start=(g == 0),
                        stop=(g == PASSES - 1),
                    )

        def exp_and_tanh(c):
            soft[c] = chan.tile([P, CHUNK_COLS], F32, name="soft", tag="soft")
            turn[c] = chan.tile([P, CHUNK_COLS], F32, name="turn", tag="turn")
            nc.scalar.activation(out=soft[c][:], in_=z_dt[c][:], func=ACT.Exp, bias=b_dt_col, scale=1.0)
            nc.scalar.activation(out=turn[c][:], in_=z_ph[c][:], func=ACT.Tanh, bias=b_ph_col, scale=1.0)
            nc.vector.tensor_scalar_min(out=soft[c][:], in0=soft[c][:], scalar1=EXP_CAP)
            nc.vector.tensor_scalar_mul(out=turn[c][:], in0=turn[c][:], scalar1=0.5)

        def b_val(c):
            z_b[c] = psum.tile([P, CHUNK_TILES, R], F32, name="z_b", tag="bank")
            for jj in range(CHUNK_TILES):
                piece = (c * CHUNK_TILES + jj) // PIECE_TILES
                j = (c * CHUNK_TILES + jj) % PIECE_TILES
                for g in range(PASSES):
                    nc.tensor.matmul_mx(
                        out=z_b[c][:, jj, :],
                        lhsT=x_codes[:, piece, g, j, :].bitcast(FP8X4),
                        lhsT_scale=x_scales[:, piece, g, j, :],
                        rhs=wb_codes[:, g, :].bitcast(FP8X4),
                        rhs_scale=wb_scales[:, g, :],
                        start=(g == 0),
                        stop=(g == PASSES - 1),
                    )

        def logarithm(c):
            nc.scalar.activation(out=soft[c][:], in_=soft[c][:], func=ACT.Ln, bias=1.0, scale=1.0)

        def step_size(c):
            nc.vector.scalar_tensor_tensor(
                out=soft[c][:], in0=z_dt[c][:], scalar=b_dt_col, in1=soft[c][:], op0=ALU.add, op1=ALU.max
            )

        def angle_in_turns(c):
            nc.vector.scalar_tensor_tensor(
                out=turn[c][:], in0=soft[c][:], scalar=turns_col[:], in1=turn[c][:], op0=ALU.mult, op1=ALU.add
            )

        def nearest_turn(c):
            frac[c] = chan.tile([P, CHUNK_COLS], F32, name="frac", tag="frac")
            nc.vector.tensor_scalar(
                out=frac[c][:], in0=turn[c][:], scalar1=ROUND_MAGIC, scalar2=ROUND_MAGIC,
                op0=ALU.add, op1=ALU.subtract,
            )

        def fraction(c):
            nc.vector.tensor_sub(out=frac[c][:], in0=frac[c][:], in1=turn[c][:])

        def sine_of(c):
            sine[c] = chan.tile([P, CHUNK_COLS], F32, name="sine", tag="sine")
            nc.scalar.activation(out=sine[c][:], in_=frac[c][:], func=ACT.Sin, scale=-2.0 * math.pi)

        def magnitude_of(c):
            cosine[c] = chan.tile([P, CHUNK_COLS], F32, name="cosine", tag="cosine")
            nc.scalar.activation(out=cosine[c][:], in_=frac[c][:], func=ACT.Abs)

        def cosine_of(c):
            nc.scalar.activation(
                out=cosine[c][:], in_=cosine[c][:], func=ACT.Sin, scale=-2.0 * math.pi, bias=math.pi / 2.0
            )

        def decay(c):
            nc.scalar.activation(out=soft[c][:], in_=soft[c][:], func=ACT.Exp, scale=neg_a_col[:])

        def back_to_rows(channel_tile):
            bank = psum.tile([P, CHUNK_TILES, R], F32, name="row_bank", tag="bank")
            for jj in range(CHUNK_TILES):
                nc.tensor.transpose(bank[:, jj, :], channel_tile[:, jj * P : (jj + 1) * P], ident[:])
            return bank

        def rotate(c):
            t0 = c * CHUNK_TILES
            sr = st_re[:, t0 : t0 + CHUNK_TILES, :]
            si = st_im[:, t0 : t0 + CHUNK_TILES, :]
            sin_t = back_to_rows(sine[c])
            cos_t = back_to_rows(cosine[c])
            re_sin = rows.tile([P, CHUNK_TILES, R], F32, tag="re_sin")
            im_sin = rows.tile([P, CHUNK_TILES, R], F32, tag="im_sin")
            re_cos = rows.tile([P, CHUNK_TILES, R], F32, tag="re_cos")
            im_cos = rows.tile([P, CHUNK_TILES, R], F32, tag="im_cos")
            nc.vector.tensor_mul(out=re_sin[:], in0=sr, in1=sin_t[:])
            nc.vector.tensor_mul(out=im_sin[:], in0=si, in1=sin_t[:])
            nc.vector.tensor_mul(out=re_cos[:], in0=sr, in1=cos_t[:])
            nc.vector.tensor_mul(out=im_cos[:], in0=si, in1=cos_t[:])
            nc.gpsimd.tensor_add(out=re_sin[:], in0=re_sin[:], in1=im_cos[:])
            nc.gpsimd.tensor_sub(out=re_cos[:], in0=re_cos[:], in1=im_sin[:])
            im_part[c] = re_sin
            re_part[c] = re_cos

        def damp_and_store(c):
            t0 = c * CHUNK_TILES
            decay_t = back_to_rows(soft[c])
            nc.vector.tensor_mul(out=re_part[c][:], in0=re_part[c][:], in1=decay_t[:])
            nc.vector.tensor_mul(out=im_part[c][:], in0=im_part[c][:], in1=decay_t[:])
            nc.sync.dma_start(out=im_rows[:, t0 : t0 + CHUNK_TILES, :], in_=im_part[c][:])
            nc.vector.tensor_add(out=re_part[c][:], in0=re_part[c][:], in1=z_b[c][:])
            nc.sync.dma_start(out=re_rows[:, t0 : t0 + CHUNK_TILES, :], in_=re_part[c][:])

        def angles(abreast):
            for c in abreast:
                step_size(c)
            for c in abreast:
                angle_in_turns(c)
            for c in abreast:
                nearest_turn(c)
            for c in abreast:
                fraction(c)

        first_half = range(0, CHUNKS // 2)
        second_half = range(CHUNKS // 2, CHUNKS)

        for piece in range(PIECES):
            quantise(piece, transposes_and_copies(x_sb[piece][:].bitcast(F32), PIECE_TILES, SCALAR_BANKS))
            behind = piece - PRODUCT_LAG
            if 0 <= behind < PIECES // 2:
                products(behind)
                if behind % PIECES_PER_CHUNK == PIECES_PER_CHUNK - 1:
                    exp_and_tanh(behind // PIECES_PER_CHUNK)

        for c in first_half:
            logarithm(c)
        wb_grouped = transposes_and_copies(w_words[:, 2:3, :], 1, 0)
        nc.vector.quantize_mx(
            out=wb_codes[:].rearrange("q g r -> q (g r)").bitcast(FP8X4),
            scales=wb_scales[:].rearrange("q g r -> q (g r)"),
            in_=wb_grouped[:],
        )
        for piece in range(PIECES // 2, PIECES):
            products(piece)
        angles(first_half)
        for c in second_half:
            exp_and_tanh(c)
        for c in range(CHUNKS):
            b_val(c)
        for c in second_half:
            logarithm(c)
        angles(second_half)

        for first in range(0, CHUNKS, ABREAST):
            abreast = range(first, first + ABREAST)
            for c in abreast:
                sine_of(c)
            for c in abreast:
                magnitude_of(c)
            for c in abreast:
                cosine_of(c)
        for c in range(CHUNKS):
            decay(c)
        for c in range(CHUNKS):
            rotate(c)
        for c in range(CHUNKS):
            damp_and_store(c)
